import numpy as np
import ml_dtypes


def mxq(x, axis, fmt="e4m3"):
    dtype, down = {"e4m3": (ml_dtypes.float8_e4m3fn, 7), "e5m2": (ml_dtypes.float8_e5m2, 14)}[fmt]
    v = np.moveaxis(np.asarray(x, np.float32).astype(ml_dtypes.bfloat16).astype(np.float64), axis, -1)
    blocks = v.reshape(v.shape[:-1] + (-1, 32))
    amax = np.abs(blocks).max(-1, keepdims=True)
    byte = np.maximum(np.where(amax > 0, np.frexp(amax)[1] - 1 + 127, 0) - down, 1)
    scale = np.exp2(byte - 127.0)
    codes = (blocks / scale).astype(np.float32).astype(dtype).astype(np.float64)
    return np.moveaxis((codes * scale).reshape(v.shape), -1, axis)


WIDE = False


def mx_kscale(k):
    if not WIDE:
        return np.ones(k)
    levels = np.array([10, -10, 5, -5, 0])
    a = np.random.permutation(np.resize(levels, k // 512 * 4)).reshape(k // 512, 4)
    idx = np.arange(k)
    return np.exp2(a[idx // 512, idx % 128 // 32])


BF16 = ml_dtypes.bfloat16


def bf(x):
    return np.asarray(x, np.float32).astype(BF16)


def f64(x):
    return np.asarray(x).astype(np.float64)


B, C, D, MIP, HH, WW = 4, 1024, 128, 32, 16, 32
N = HH * WW


def sigmoid(v):
    return 1.0 / (1.0 + np.exp(-v))


def setup_inputs():
    s = mx_kscale(C)
    return {"x": bf(np.random.standard_normal((B, C, HH, WW)) * s[None, :, None, None]),
            "q_w": bf(np.random.standard_normal((D, C)) * 0.6 / np.sqrt(C) / s[None, :]),
            "q_b": bf(np.random.standard_normal(D) * 0.1),
            "k_w": bf(np.random.standard_normal((D, C)) * 0.6 / np.sqrt(C) / s[None, :]),
            "k_b": bf(np.random.standard_normal(D) * 0.1),
            "a_h": bf(sigmoid(np.random.standard_normal((B, D, HH))) / s[None, :D, None]),
            "a_w": bf(sigmoid(np.random.standard_normal((B, D, WW))))}


def reference(x, q_w, q_b, k_w, k_b, a_h, a_w):
    x4 = f64(x)
    xq = mxq(x4.reshape(B, C, N), 1, "e4m3")
    q = ((mxq(f64(q_w), 1, "e4m3") @ xq) + f64(q_b)[None, :, None]).transpose(0, 2, 1)
    k = (mxq(f64(k_w), 1, "e4m3") @ xq) + f64(k_b)[None, :, None]
    bias = (f64(a_w)[:, :, None, :] * f64(a_h)[:, :, :, None] * x4[:, :D]).reshape(B, D, N)
    return q, k + bias

@@ -1,0 +1,169 @@
+from contextlib import ExitStack
+
+import concourse.mybir as mybir
+from concourse.masks import make_identity
+
+F32 = mybir.dt.float32
+BF16 = mybir.dt.bfloat16
+U32 = mybir.dt.uint32
+U8 = mybir.dt.uint8
+FP8X4 = mybir.dt.float8_e4m3fn_x4
+ADD = mybir.AluOpType.add
+MULT = mybir.AluOpType.mult
+
+P = 128
+PACK = 4
+K_PASS = P * PACK
+B, C, D, HH, WW = 4, 1024, 128, 16, 32
+N = HH * WW
+PASSES = C // K_PASS
+N_TILES = N // P
+HALVES = 2
+RUN = 4
+QW, KW = 0, 1
+VECTOR_PIXELS = 64
+
+FLOPS = 2 * 2 * B * N * D * C
+
+
+def regroup(copy, grouped, raw, pixels):
+    copy(
+        out=grouped[:, pixels, :].rearrange("p (c i) t -> p c t i", i=RUN),
+        in_=raw[:, :, pixels].rearrange("p t (c i) -> p c t i", i=RUN),
+    )
+
+
+def tile_self_attn_pa_kernel(tc, x, q_w, q_b, k_w, k_b, a_h, a_w, out_0, out_1):
+    nc = tc.nc
+    steps = [(b, g) for b in range(B) for g in range(PASSES)]
+    with ExitStack() as ctx:
+        keep = ctx.enter_context(tc.tile_pool(name="keep", bufs=1))
+        per_step = ctx.enter_context(tc.tile_pool(name="per_step", bufs=len(steps)))
+        per_image = ctx.enter_context(tc.tile_pool(name="per_image", bufs=B))
+        psum_w = ctx.enter_context(tc.psum_pool(name="psum_w", bufs=2))
+        psum_q = ctx.enter_context(tc.psum_pool(name="psum_q", bufs=3))
+        psum_k = ctx.enter_context(tc.psum_pool(name="psum_k", bufs=3))
+
+        gate_h = keep.tile([P, B, HH], BF16)
+        nc.scalar.dma_start(out=gate_h[:], in_=a_h.rearrange("b d i -> d b i"))
+        gate_w = keep.tile([P, B, WW], BF16)
+        nc.scalar.dma_start(out=gate_w[:], in_=a_w.rearrange("b d j -> d b j"))
+        k_bias_bf = keep.tile([P, 1], BF16)
+        nc.scalar.dma_start(out=k_bias_bf[:], in_=k_b.rearrange("(d o) -> d o", o=1))
+        q_bias = keep.tile([P, D], BF16)
+        nc.scalar.dma_start(out=q_bias[:], in_=q_b.partition_broadcast(P))
+
+        def load_pass(b, g):
+            raw = per_step.tile([P, PACK, N], BF16, name="raw")
+            channels = x[b, g * K_PASS : (g + 1) * K_PASS]
+            nc.sync.dma_start(out=raw[:], in_=channels.rearrange("(p t) h w -> p t (h w)", t=PACK))
+            return raw
+
+        raws = [load_pass(*steps[0])]
+        q_w_rows = keep.tile([P, C], BF16)
+        nc.sync.dma_start(out=q_w_rows[:], in_=q_w)
+        k_w_rows = keep.tile([P, C], BF16)
+        nc.sync.dma_start(out=k_w_rows[:], in_=k_w)
+        raws.append(load_pass(*steps[1]))
+        first_channels = keep.tile([P, B, N], BF16)
+        nc.sync.dma_start(out=first_channels[:], in_=x[:, 0:D].rearrange("b d h w -> d b (h w)"))
+        for b, g in steps[2:]:
+            raws.append(load_pass(b, g))
+
+        gate = keep.tile([P, B, HH, WW], F32)
+        nc.vector.tensor_tensor(
+            out=gate[:],
+            in0=gate_h[:].unsqueeze(3).to_broadcast([P, B, HH, WW]),
+            in1=gate_w[:].unsqueeze(2).to_broadcast([P, B, HH, WW]),
+            op=MULT,
+        )
+        k_bias = keep.tile([P, 1], F32)
+        nc.vector.tensor_copy(out=k_bias[:], in_=k_bias_bf[:])
+
+        identity = keep.tile([P, P], F32)
+        make_identity(nc, identity[:])
+        w_grouped = keep.tile([P, 2 * PASSES * D * PACK], BF16, align_bytes=64)
+        w_grouped_words = w_grouped[:].bitcast(F32).rearrange(
+            "p (w g d u) -> p w g d u", w=2, g=PASSES, u=HALVES
+        )
+
+        def transpose_weight(rows, place, copy):
+            words = rows[:].bitcast(F32).rearrange("d (g p u) -> d g u p", g=PASSES, u=HALVES)
+            w_t = psum_w.tile([P, PASSES, HALVES, D], F32)
+            for g in range(PASSES):
+                for u in range(HALVES):
+                    nc.tensor.transpose(w_t[:, g, u, :], words[:, g, u, :], identity[:])
+            copy(out=w_grouped_words[:, place], in_=w_t[:].rearrange("p g u d -> p g d u"))
+
+        transpose_weight(q_w_rows, QW, nc.scalar.copy)
+        transpose_weight(k_w_rows, KW, nc.vector.tensor_copy)
+        w_codes = keep.tile([P, 2, PASSES, D], U32, align_bytes=64)
+        w_scales = keep.tile([P, 2, PASSES, D], U8, align_bytes=64)
+        nc.vector.quantize_mx(
+            out=w_codes[:].rearrange("p w g d -> p (w g d)").bitcast(FP8X4),
+            scales=w_scales[:].rearrange("p w g d -> p (w g d)"),
+            in_=w_grouped[:],
+        )
+
+        for b in range(B):
+            k_acc = psum_k.tile([P, N], F32)
+            x_codes = []
+            x_scales = []
+            for g in range(PASSES):
+                raw = raws[b * PASSES + g]
+                grouped = per_step.tile([P, N, PACK], BF16, align_bytes=64)
+                regroup(nc.vector.tensor_copy, grouped, raw, slice(0, VECTOR_PIXELS))
+                regroup(nc.scalar.copy, grouped, raw, slice(VECTOR_PIXELS, N))
+                codes = per_step.tile([P, N], U32, align_bytes=64)
+                scales = per_step.tile([P, N], U8, align_bytes=64)
+                nc.vector.quantize_mx(
+                    out=codes[:].bitcast(FP8X4),
+                    scales=scales[:],
+                    in_=grouped[:].rearrange("p n t -> p (n t)"),
+                )
+                x_codes.append(codes)
+                x_scales.append(scales)
+                nc.tensor.matmul_mx(
+                    out=k_acc[:],
+                    lhsT=w_codes[:, KW, g, :].bitcast(FP8X4),
+                    lhsT_scale=w_scales[:, KW, g, :],
+                    rhs=codes[:].bitcast(FP8X4),
+                    rhs_scale=scales[:],
+                    start=(g == 0),
+                    stop=(g == PASSES - 1),
+                )
+
+            q_acc = psum_q.tile([P, N_TILES, D], F32)
+            for s in range(N_TILES):
+                pixels = slice(s * P, (s + 1) * P)
+                for g in range(PASSES):
+                    nc.tensor.matmul_mx(
+                        out=q_acc[:, s, :],
+                        lhsT=x_codes[g][:, pixels].bitcast(FP8X4),
+                        lhsT_scale=x_scales[g][:, pixels],
+                        rhs=w_codes[:, QW, g, :].bitcast(FP8X4),
+                        rhs_scale=w_scales[:, QW, g, :],
+                        start=(g == 0),
+                        stop=(g == PASSES - 1),
+                    )
+            q_out = per_image.tile([P, N_TILES, D], F32)
+            nc.vector.tensor_tensor(
+                out=q_out[:],
+                in0=q_acc[:],
+                in1=q_bias[:].unsqueeze(1).to_broadcast([P, N_TILES, D]),
+                op=ADD,
+            )
+            nc.sync.dma_start(out=out_0[b].rearrange("(s p) d -> p s d", p=P), in_=q_out[:])
+
+            gated = per_image.tile([P, N], F32)
+            nc.vector.tensor_tensor(
+                out=gated[:],
+                in0=first_channels[:, b, :],
+                in1=gate[:, b].rearrange("p i j -> p (i j)"),
+                op=MULT,
+            )
+            k_out = per_image.tile([P, N], F32)
+            nc.vector.scalar_tensor_tensor(
+                out=k_out[:], in0=k_acc[:], scalar=k_bias[:, 0:1], in1=gated[:], op0=ADD, op1=ADD
+            )
+            nc.sync.dma_start(out=out_1[b], in_=k_out[:])

@@ -17,59 +17,146 @@ K_PASS = P * PACK
 B, C, D, HH, WW = 4, 1024, 128, 16, 32
 N = HH * WW
 PASSES = C // K_PASS
+STEPS = B * PASSES
 N_TILES = N // P
 HALVES = 2
 RUN = 4
 QW, KW = 0, 1
-VECTOR_PIXELS = 64
+VECTOR_PIXELS = 96
 
 FLOPS = 2 * 2 * B * N * D * C
 
 
-def regroup(copy, grouped, raw, pixels):
-    copy(
-        out=grouped[:, pixels, :].rearrange("p (c i) t -> p c t i", i=RUN),
-        in_=raw[:, :, pixels].rearrange("p t (c i) -> p c t i", i=RUN),
-    )
-
-
 def tile_self_attn_pa_kernel(tc, x, q_w, q_b, k_w, k_b, a_h, a_w, out_0, out_1):
     nc = tc.nc
-    steps = [(b, g) for b in range(B) for g in range(PASSES)]
     with ExitStack() as ctx:
         keep = ctx.enter_context(tc.tile_pool(name="keep", bufs=1))
-        per_step = ctx.enter_context(tc.tile_pool(name="per_step", bufs=len(steps)))
+        per_step = ctx.enter_context(tc.tile_pool(name="per_step", bufs=STEPS))
         per_image = ctx.enter_context(tc.tile_pool(name="per_image", bufs=B))
         psum_w = ctx.enter_context(tc.psum_pool(name="psum_w", bufs=2))
         psum_q = ctx.enter_context(tc.psum_pool(name="psum_q", bufs=3))
         psum_k = ctx.enter_context(tc.psum_pool(name="psum_k", bufs=3))
 
-        gate_h = keep.tile([P, B, HH], BF16)
-        nc.scalar.dma_start(out=gate_h[:], in_=a_h.rearrange("b d i -> d b i"))
-        gate_w = keep.tile([P, B, WW], BF16)
-        nc.scalar.dma_start(out=gate_w[:], in_=a_w.rearrange("b d j -> d b j"))
-        k_bias_bf = keep.tile([P, 1], BF16)
-        nc.scalar.dma_start(out=k_bias_bf[:], in_=k_b.rearrange("(d o) -> d o", o=1))
-        q_bias = keep.tile([P, D], BF16)
-        nc.scalar.dma_start(out=q_bias[:], in_=q_b.partition_broadcast(P))
+        raws = []
 
-        def load_pass(b, g):
+        def load_pass():
+            b, g = divmod(len(raws), PASSES)
             raw = per_step.tile([P, PACK, N], BF16, name="raw")
             channels = x[b, g * K_PASS : (g + 1) * K_PASS]
             nc.sync.dma_start(out=raw[:], in_=channels.rearrange("(p t) h w -> p t (h w)", t=PACK))
-            return raw
+            raws.append(raw)
 
-        raws = [load_pass(*steps[0])]
+        load_pass()
+        gate_h = keep.tile([P, B, HH], BF16)
+        nc.sync.dma_start(out=gate_h[:], in_=a_h.rearrange("b d i -> d b i"))
+        gate_w = keep.tile([P, B, WW], BF16)
+        nc.sync.dma_start(out=gate_w[:], in_=a_w.rearrange("b d j -> d b j"))
+        load_pass()
         q_w_rows = keep.tile([P, C], BF16)
         nc.sync.dma_start(out=q_w_rows[:], in_=q_w)
         k_w_rows = keep.tile([P, C], BF16)
         nc.sync.dma_start(out=k_w_rows[:], in_=k_w)
-        raws.append(load_pass(*steps[1]))
+        load_pass()
         first_channels = keep.tile([P, B, N], BF16)
         nc.sync.dma_start(out=first_channels[:], in_=x[:, 0:D].rearrange("b d h w -> d b (h w)"))
-        for b, g in steps[2:]:
-            raws.append(load_pass(b, g))
+        load_pass()
+        k_bias = keep.tile([P, 1], BF16)
+        nc.sync.dma_start(out=k_bias[:], in_=k_b.rearrange("(d o) -> d o", o=1))
+        q_bias = keep.tile([P, D], BF16)
+        nc.sync.dma_start(out=q_bias[:], in_=q_b.partition_broadcast(P))
+        for c in range(len(raws), STEPS):
+            load_pass()
 
+        identity = keep.tile([P, P], F32)
+        make_identity(nc, identity[:])
+
+        groupeds = []
+        x_codes = []
+        x_scales = []
+        k_accs = []
+        q_accs = []
+        w_codes = keep.tile([P, 2, PASSES, D], U32, align_bytes=64)
+        w_scales = keep.tile([P, 2, PASSES, D], U8, align_bytes=64)
+
+        def regroup(c):
+            grouped = per_step.tile([P, N, PACK], BF16, align_bytes=64, name="grouped")
+            for copy, pixels in (
+                (nc.vector.tensor_copy, slice(0, VECTOR_PIXELS)),
+                (nc.scalar.copy, slice(VECTOR_PIXELS, N)),
+            ):
+                copy(
+                    out=grouped[:, pixels, :].rearrange("p (c i) t -> p c t i", i=RUN),
+                    in_=raws[c][:, :, pixels].rearrange("p t (c i) -> p c t i", i=RUN),
+                )
+            groupeds.append(grouped)
+
+        def quantise(c):
+            codes = per_step.tile([P, N], U32, align_bytes=64, name="codes")
+            scales = per_step.tile([P, N], U8, align_bytes=64, name="scales")
+            nc.vector.quantize_mx(
+                out=codes[:].bitcast(FP8X4),
+                scales=scales[:],
+                in_=groupeds[c][:].rearrange("p n t -> p (n t)"),
+            )
+            x_codes.append(codes)
+            x_scales.append(scales)
+
+        def project(c):
+            b, g = divmod(c, PASSES)
+            if g == 0:
+                k_accs.append(psum_k.tile([P, N], F32, name="k_acc"))
+            nc.tensor.matmul_mx(
+                out=k_accs[b][:],
+                lhsT=w_codes[:, KW, g, :].bitcast(FP8X4),
+                lhsT_scale=w_scales[:, KW, g, :],
+                rhs=x_codes[c][:].bitcast(FP8X4),
+                rhs_scale=x_scales[c][:],
+                start=(g == 0),
+                stop=(g == PASSES - 1),
+            )
+            if g < PASSES - 1:
+                return
+            q_acc = psum_q.tile([P, N_TILES, D], F32, name="q_acc")
+            for s in range(N_TILES):
+                pixels = slice(s * P, (s + 1) * P)
+                for h in range(PASSES):
+                    nc.tensor.matmul_mx(
+                        out=q_acc[:, s, :],
+                        lhsT=x_codes[b * PASSES + h][:, pixels].bitcast(FP8X4),
+                        lhsT_scale=x_scales[b * PASSES + h][:, pixels],
+                        rhs=w_codes[:, QW, h, :].bitcast(FP8X4),
+                        rhs_scale=w_scales[:, QW, h, :],
+                        start=(h == 0),
+                        stop=(h == PASSES - 1),
+                    )
+            q_accs.append(q_acc)
+
+        def finish(c):
+            b, g = divmod(c, PASSES)
+            if g < PASSES - 1:
+                return
+            q_out = per_image.tile([P, N_TILES, D], F32, name="q_out")
+            nc.vector.tensor_tensor(
+                out=q_out[:],
+                in0=q_accs[b][:],
+                in1=q_bias[:].unsqueeze(1).to_broadcast([P, N_TILES, D]),
+                op=ADD,
+            )
+            nc.sync.dma_start(out=out_0[b].rearrange("(s p) d -> p s d", p=P), in_=q_out[:])
+            gated = per_image.tile([P, N], F32, name="gated")
+            nc.vector.tensor_tensor(
+                out=gated[:],
+                in0=first_channels[:, b, :],
+                in1=gate[:, b].rearrange("p i j -> p (i j)"),
+                op=MULT,
+            )
+            k_out = per_image.tile([P, N], F32, name="k_out")
+            nc.vector.scalar_tensor_tensor(
+                out=k_out[:], in0=k_accs[b][:], scalar=k_bias[:, 0:1], in1=gated[:], op0=ADD, op1=ADD
+            )
+            nc.sync.dma_start(out=out_1[b], in_=k_out[:])
+
+        regroup(0)
         gate = keep.tile([P, B, HH, WW], F32)
         nc.vector.tensor_tensor(
             out=gate[:],
@@ -77,93 +164,32 @@ def tile_self_attn_pa_kernel(tc, x, q_w, q_b, k_w, k_b, a_h, a_w, out_0, out_1):
             in1=gate_w[:].unsqueeze(2).to_broadcast([P, B, HH, WW]),
             op=MULT,
         )
-        k_bias = keep.tile([P, 1], F32)
-        nc.vector.tensor_copy(out=k_bias[:], in_=k_bias_bf[:])
+        regroup(1)
+        quantise(0)
 
-        identity = keep.tile([P, P], F32)
-        make_identity(nc, identity[:])
         w_grouped = keep.tile([P, 2 * PASSES * D * PACK], BF16, align_bytes=64)
         w_grouped_words = w_grouped[:].bitcast(F32).rearrange(
             "p (w g d u) -> p w g d u", w=2, g=PASSES, u=HALVES
         )
-
-        def transpose_weight(rows, place, copy):
+        for rows, place, copy in ((q_w_rows, QW, nc.scalar.copy), (k_w_rows, KW, nc.vector.tensor_copy)):
             words = rows[:].bitcast(F32).rearrange("d (g p u) -> d g u p", g=PASSES, u=HALVES)
-            w_t = psum_w.tile([P, PASSES, HALVES, D], F32)
+            w_t = psum_w.tile([P, PASSES, HALVES, D], F32, name="w_t")
             for g in range(PASSES):
                 for u in range(HALVES):
                     nc.tensor.transpose(w_t[:, g, u, :], words[:, g, u, :], identity[:])
             copy(out=w_grouped_words[:, place], in_=w_t[:].rearrange("p g u d -> p g d u"))
-
-        transpose_weight(q_w_rows, QW, nc.scalar.copy)
-        transpose_weight(k_w_rows, KW, nc.vector.tensor_copy)
-        w_codes = keep.tile([P, 2, PASSES, D], U32, align_bytes=64)
-        w_scales = keep.tile([P, 2, PASSES, D], U8, align_bytes=64)
         nc.vector.quantize_mx(
             out=w_codes[:].rearrange("p w g d -> p (w g d)").bitcast(FP8X4),
             scales=w_scales[:].rearrange("p w g d -> p (w g d)"),
             in_=w_grouped[:],
         )
 
-        for b in range(B):
-            k_acc = psum_k.tile([P, N], F32)
-            x_codes = []
-            x_scales = []
-            for g in range(PASSES):
-                raw = raws[b * PASSES + g]
-                grouped = per_step.tile([P, N, PACK], BF16, align_bytes=64)
-                regroup(nc.vector.tensor_copy, grouped, raw, slice(0, VECTOR_PIXELS))
-                regroup(nc.scalar.copy, grouped, raw, slice(VECTOR_PIXELS, N))
-                codes = per_step.tile([P, N], U32, align_bytes=64)
-                scales = per_step.tile([P, N], U8, align_bytes=64)
-                nc.vector.quantize_mx(
-                    out=codes[:].bitcast(FP8X4),
-                    scales=scales[:],
-                    in_=grouped[:].rearrange("p n t -> p (n t)"),
-                )
-                x_codes.append(codes)
-                x_scales.append(scales)
-                nc.tensor.matmul_mx(
-                    out=k_acc[:],
-                    lhsT=w_codes[:, KW, g, :].bitcast(FP8X4),
-                    lhsT_scale=w_scales[:, KW, g, :],
-                    rhs=codes[:].bitcast(FP8X4),
-                    rhs_scale=scales[:],
-                    start=(g == 0),
-                    stop=(g == PASSES - 1),
-                )
-
-            q_acc = psum_q.tile([P, N_TILES, D], F32)
-            for s in range(N_TILES):
-                pixels = slice(s * P, (s + 1) * P)
-                for g in range(PASSES):
-                    nc.tensor.matmul_mx(
-                        out=q_acc[:, s, :],
-                        lhsT=x_codes[g][:, pixels].bitcast(FP8X4),
-                        lhsT_scale=x_scales[g][:, pixels],
-                        rhs=w_codes[:, QW, g, :].bitcast(FP8X4),
-                        rhs_scale=w_scales[:, QW, g, :],
-                        start=(g == 0),
-                        stop=(g == PASSES - 1),
-                    )
-            q_out = per_image.tile([P, N_TILES, D], F32)
-            nc.vector.tensor_tensor(
-                out=q_out[:],
-                in0=q_acc[:],
-                in1=q_bias[:].unsqueeze(1).to_broadcast([P, N_TILES, D]),
-                op=ADD,
-            )
-            nc.sync.dma_start(out=out_0[b].rearrange("(s p) d -> p s d", p=P), in_=q_out[:])
-
-            gated = per_image.tile([P, N], F32)
-            nc.vector.tensor_tensor(
-                out=gated[:],
-                in0=first_channels[:, b, :],
-                in1=gate[:, b].rearrange("p i j -> p (i j)"),
-                op=MULT,
-            )
-            k_out = per_image.tile([P, N], F32)
-            nc.vector.scalar_tensor_tensor(
-                out=k_out[:], in0=k_acc[:], scalar=k_bias[:, 0:1], in1=gated[:], op0=ADD, op1=ADD
-            )
-            nc.sync.dma_start(out=out_1[b], in_=k_out[:])
+        for c in range(2, STEPS + 3):
+            if c < STEPS:
+                regroup(c)
+            if c - 1 < STEPS:
+                quantise(c - 1)
+            if c - 2 < STEPS:
+                project(c - 2)
+            if c - 3 >= 0:
+                finish(c - 3)

@@ -30,6 +30,7 @@ FLOPS = 2 * 2 * B * N * D * C
 def tile_self_attn_pa_kernel(tc, x, q_w, q_b, k_w, k_b, a_h, a_w, out_0, out_1):
     nc = tc.nc
     with ExitStack() as ctx:
+        ctx.enter_context(tc.manual_schedule())
         keep = ctx.enter_context(tc.tile_pool(name="keep", bufs=1))
         per_step = ctx.enter_context(tc.tile_pool(name="per_step", bufs=STEPS))
         per_image = ctx.enter_context(tc.tile_pool(name="per_image", bufs=B))

@@ -30,12 +30,12 @@ FLOPS = 2 * 2 * B * N * D * C
 def tile_self_attn_pa_kernel(tc, x, q_w, q_b, k_w, k_b, a_h, a_w, out_0, out_1):
     nc = tc.nc
     with ExitStack() as ctx:
-        ctx.enter_context(tc.manual_schedule())
         keep = ctx.enter_context(tc.tile_pool(name="keep", bufs=1))
         per_step = ctx.enter_context(tc.tile_pool(name="per_step", bufs=STEPS))
         per_image = ctx.enter_context(tc.tile_pool(name="per_image", bufs=B))
         psum_w = ctx.enter_context(tc.psum_pool(name="psum_w", bufs=2))
-        psum_q = ctx.enter_context(tc.psum_pool(name="psum_q", bufs=3))
+        psum_b = ctx.enter_context(tc.psum_pool(name="psum_b", bufs=1))
+        psum_q = ctx.enter_context(tc.psum_pool(name="psum_q", bufs=2))
         psum_k = ctx.enter_context(tc.psum_pool(name="psum_k", bufs=3))
 
         raws = []
@@ -52,6 +52,10 @@ def tile_self_attn_pa_kernel(tc, x, q_w, q_b, k_w, k_b, a_h, a_w, out_0, out_1):
         nc.sync.dma_start(out=gate_h[:], in_=a_h.rearrange("b d i -> d b i"))
         gate_w = keep.tile([P, B, WW], BF16)
         nc.sync.dma_start(out=gate_w[:], in_=a_w.rearrange("b d j -> d b j"))
+        bias_rows = keep.tile([P, 2, D], BF16)
+        nc.gpsimd.memset(bias_rows[:], 0.0)
+        nc.sync.dma_start(out=bias_rows[0:1, QW, :], in_=q_b.rearrange("(o d) -> o d", o=1))
+        nc.sync.dma_start(out=bias_rows[0:1, KW, :], in_=k_b.rearrange("(o d) -> o d", o=1))
         load_pass()
         q_w_rows = keep.tile([P, C], BF16)
         nc.sync.dma_start(out=q_w_rows[:], in_=q_w)
@@ -61,15 +65,21 @@ def tile_self_attn_pa_kernel(tc, x, q_w, q_b, k_w, k_b, a_h, a_w, out_0, out_1):
         first_channels = keep.tile([P, B, N], BF16)
         nc.sync.dma_start(out=first_channels[:], in_=x[:, 0:D].rearrange("b d h w -> d b (h w)"))
         load_pass()
-        k_bias = keep.tile([P, 1], BF16)
-        nc.sync.dma_start(out=k_bias[:], in_=k_b.rearrange("(d o) -> d o", o=1))
-        q_bias = keep.tile([P, D], BF16)
-        nc.sync.dma_start(out=q_bias[:], in_=q_b.partition_broadcast(P))
         for c in range(len(raws), STEPS):
             load_pass()
 
         identity = keep.tile([P, P], F32)
         make_identity(nc, identity[:])
+
+        ones = keep.tile([P, P], BF16)
+        nc.gpsimd.memset(ones[:], 1.0)
+        bias_acc = psum_b.tile([P, 2, D], F32)
+        nc.tensor.matmul(out=bias_acc[:, QW, :], lhsT=ones[:], rhs=bias_rows[:, QW, :], start=True, stop=True)
+        nc.tensor.matmul(out=bias_acc[:, KW, :], lhsT=bias_rows[:, KW, :], rhs=ones[:], start=True, stop=True)
+        biases = keep.tile([P, 2, D], F32)
+        nc.scalar.copy(out=biases[:], in_=bias_acc[:])
+        q_bias = biases[:, QW, :]
+        k_bias = biases[:, KW, 0:1]
 
         groupeds = []
         x_codes = []
@@ -140,7 +150,7 @@ def tile_self_attn_pa_kernel(tc, x, q_w, q_b, k_w, k_b, a_h, a_w, out_0, out_1):
             nc.vector.tensor_tensor(
                 out=q_out[:],
                 in0=q_accs[b][:],
-                in1=q_bias[:].unsqueeze(1).to_broadcast([P, N_TILES, D]),
+                in1=q_bias.unsqueeze(1).to_broadcast([P, N_TILES, D]),
                 op=ADD,
             )
             nc.sync.dma_start(out=out_0[b].rearrange("(s p) d -> p s d", p=P), in_=q_out[:])
@@ -153,7 +163,7 @@ def tile_self_attn_pa_kernel(tc, x, q_w, q_b, k_w, k_b, a_h, a_w, out_0, out_1):
             )
             k_out = per_image.tile([P, N], F32, name="k_out")
             nc.vector.scalar_tensor_tensor(
-                out=k_out[:], in0=k_accs[b][:], scalar=k_bias[:, 0:1], in1=gated[:], op0=ADD, op1=ADD
+                out=k_out[:], in0=k_accs[b][:], scalar=k_bias, in1=gated[:], op0=ADD, op1=ADD
             )
             nc.sync.dma_start(out=out_1[b], in_=k_out[:])
 

@@ -22,7 +22,7 @@ N_TILES = N // P
 HALVES = 2
 RUN = 4
 QW, KW = 0, 1
-VECTOR_PIXELS = 96
+VECTOR_PIXELS = 128
 
 FLOPS = 2 * 2 * B * N * D * C
 
@@ -146,6 +146,11 @@ def tile_self_attn_pa_kernel(tc, x, q_w, q_b, k_w, k_b, a_h, a_w, out_0, out_1):
             b, g = divmod(c, PASSES)
             if g < PASSES - 1:
                 return
+            k_out = per_image.tile([P, N], F32, name="k_out")
+            nc.vector.scalar_tensor_tensor(
+                out=k_out[:], in0=k_accs[b][:], scalar=k_bias, in1=gated[:, b, :], op0=ADD, op1=ADD
+            )
+            nc.sync.dma_start(out=out_1[b], in_=k_out[:])
             q_out = per_image.tile([P, N_TILES, D], F32, name="q_out")
             nc.vector.tensor_tensor(
                 out=q_out[:],
@@ -154,18 +159,6 @@ def tile_self_attn_pa_kernel(tc, x, q_w, q_b, k_w, k_b, a_h, a_w, out_0, out_1):
                 op=ADD,
             )
             nc.sync.dma_start(out=out_0[b].rearrange("(s p) d -> p s d", p=P), in_=q_out[:])
-            gated = per_image.tile([P, N], F32, name="gated")
-            nc.vector.tensor_tensor(
-                out=gated[:],
-                in0=first_channels[:, b, :],
-                in1=gate[:, b].rearrange("p i j -> p (i j)"),
-                op=MULT,
-            )
-            k_out = per_image.tile([P, N], F32, name="k_out")
-            nc.vector.scalar_tensor_tensor(
-                out=k_out[:], in0=k_accs[b][:], scalar=k_bias, in1=gated[:], op0=ADD, op1=ADD
-            )
-            nc.sync.dma_start(out=out_1[b], in_=k_out[:])
 
         regroup(0)
         gate = keep.tile([P, B, HH, WW], F32)
@@ -182,7 +175,7 @@ def tile_self_attn_pa_kernel(tc, x, q_w, q_b, k_w, k_b, a_h, a_w, out_0, out_1):
         w_grouped_words = w_grouped[:].bitcast(F32).rearrange(
             "p (w g d u) -> p w g d u", w=2, g=PASSES, u=HALVES
         )
-        for rows, place, copy in ((q_w_rows, QW, nc.scalar.copy), (k_w_rows, KW, nc.vector.tensor_copy)):
+        for rows, place, copy in ((q_w_rows, QW, nc.scalar.copy), (k_w_rows, KW, nc.scalar.copy)):
             words = rows[:].bitcast(F32).rearrange("d (g p u) -> d g u p", g=PASSES, u=HALVES)
             w_t = psum_w.tile([P, PASSES, HALVES, D], F32, name="w_t")
             for g in range(PASSES):
@@ -193,6 +186,11 @@ def tile_self_attn_pa_kernel(tc, x, q_w, q_b, k_w, k_b, a_h, a_w, out_0, out_1):
             out=w_codes[:].rearrange("p w g d -> p (w g d)").bitcast(FP8X4),
             scales=w_scales[:].rearrange("p w g d -> p (w g d)"),
             in_=w_grouped[:],
+        )
+
+        gated = keep.tile([P, B, N], F32)
+        nc.vector.tensor_tensor(
+            out=gated[:], in0=first_channels[:], in1=gate[:].rearrange("p b i j -> p b (i j)"), op=MULT
         )
 
         for c in range(2, STEPS + 3):

@@ -23,6 +23,8 @@ HALVES = 2
 RUN = 4
 QW, KW = 0, 1
 VECTOR_PIXELS = 128
+CUTS = {STEPS - 1: (0, N // 2, N)}
+VECTOR_SHARE = {STEPS - 1: 64, STEPS: 64}
 
 FLOPS = 2 * 2 * B * N * D * C
 
@@ -32,7 +34,7 @@ def tile_self_attn_pa_kernel(tc, x, q_w, q_b, k_w, k_b, a_h, a_w, out_0, out_1):
     with ExitStack() as ctx:
         keep = ctx.enter_context(tc.tile_pool(name="keep", bufs=1))
         per_step = ctx.enter_context(tc.tile_pool(name="per_step", bufs=STEPS))
-        per_image = ctx.enter_context(tc.tile_pool(name="per_image", bufs=B))
+        per_unit = ctx.enter_context(tc.tile_pool(name="per_unit", bufs=B + 1))
         psum_w = ctx.enter_context(tc.psum_pool(name="psum_w", bufs=2))
         psum_b = ctx.enter_context(tc.psum_pool(name="psum_b", bufs=1))
         psum_q = ctx.enter_context(tc.psum_pool(name="psum_q", bufs=2))
@@ -81,84 +83,101 @@ def tile_self_attn_pa_kernel(tc, x, q_w, q_b, k_w, k_b, a_h, a_w, out_0, out_1):
         q_bias = biases[:, QW, :]
         k_bias = biases[:, KW, 0:1]
 
+        chunks = []
+        for c in range(STEPS):
+            cuts = CUTS.get(c, (0, N))
+            chunks.extend((c, lo, hi) for lo, hi in zip(cuts[:-1], cuts[1:]))
+        units = []
+        for b in range(B):
+            cuts = CUTS.get(b * PASSES + PASSES - 1, (0, N))
+            units.extend((b, lo, hi) for lo, hi in zip(cuts[:-1], cuts[1:]))
+
         groupeds = []
         x_codes = []
         x_scales = []
-        k_accs = []
-        q_accs = []
+        for c in range(STEPS):
+            groupeds.append(per_step.tile([P, N, PACK], BF16, align_bytes=64, name="grouped"))
+            x_codes.append(per_step.tile([P, N], U32, align_bytes=64, name="codes"))
+            x_scales.append(per_step.tile([P, N], U8, align_bytes=64, name="scales"))
+        k_accs = {}
+        q_accs = {}
         w_codes = keep.tile([P, 2, PASSES, D], U32, align_bytes=64)
         w_scales = keep.tile([P, 2, PASSES, D], U8, align_bytes=64)
 
-        def regroup(c):
-            grouped = per_step.tile([P, N, PACK], BF16, align_bytes=64, name="grouped")
-            for copy, pixels in (
-                (nc.vector.tensor_copy, slice(0, VECTOR_PIXELS)),
-                (nc.scalar.copy, slice(VECTOR_PIXELS, N)),
-            ):
+        def regroup(j):
+            c, lo, hi = chunks[j]
+            cut = lo + VECTOR_SHARE.get(j, VECTOR_PIXELS)
+            for copy, pixels in ((nc.vector.tensor_copy, slice(lo, cut)), (nc.scalar.copy, slice(cut, hi))):
+                if pixels.start == pixels.stop:
+                    continue
                 copy(
-                    out=grouped[:, pixels, :].rearrange("p (c i) t -> p c t i", i=RUN),
+                    out=groupeds[c][:, pixels, :].rearrange("p (c i) t -> p c t i", i=RUN),
                     in_=raws[c][:, :, pixels].rearrange("p t (c i) -> p c t i", i=RUN),
                 )
-            groupeds.append(grouped)
 
-        def quantise(c):
-            codes = per_step.tile([P, N], U32, align_bytes=64, name="codes")
-            scales = per_step.tile([P, N], U8, align_bytes=64, name="scales")
+        def quantise(j):
+            c, lo, hi = chunks[j]
             nc.vector.quantize_mx(
-                out=codes[:].bitcast(FP8X4),
-                scales=scales[:],
-                in_=groupeds[c][:].rearrange("p n t -> p (n t)"),
+                out=x_codes[c][:, lo:hi].bitcast(FP8X4),
+                scales=x_scales[c][:, lo:hi],
+                in_=groupeds[c][:, lo:hi, :].rearrange("p n t -> p (n t)"),
             )
-            x_codes.append(codes)
-            x_scales.append(scales)
 
-        def project(c):
-            b, g = divmod(c, PASSES)
-            if g == 0:
-                k_accs.append(psum_k.tile([P, N], F32, name="k_acc"))
-            nc.tensor.matmul_mx(
-                out=k_accs[b][:],
-                lhsT=w_codes[:, KW, g, :].bitcast(FP8X4),
-                lhsT_scale=w_scales[:, KW, g, :],
-                rhs=x_codes[c][:].bitcast(FP8X4),
-                rhs_scale=x_scales[c][:],
-                start=(g == 0),
-                stop=(g == PASSES - 1),
-            )
-            if g < PASSES - 1:
-                return
-            q_acc = psum_q.tile([P, N_TILES, D], F32, name="q_acc")
-            for s in range(N_TILES):
-                pixels = slice(s * P, (s + 1) * P)
-                for h in range(PASSES):
-                    nc.tensor.matmul_mx(
-                        out=q_acc[:, s, :],
-                        lhsT=x_codes[b * PASSES + h][:, pixels].bitcast(FP8X4),
-                        lhsT_scale=x_scales[b * PASSES + h][:, pixels],
-                        rhs=w_codes[:, QW, h, :].bitcast(FP8X4),
-                        rhs_scale=w_scales[:, QW, h, :],
-                        start=(h == 0),
-                        stop=(h == PASSES - 1),
-                    )
-            q_accs.append(q_acc)
+        def units_of(j):
+            c, lo, hi = chunks[j]
+            return [u for u in units if u[0] == c // PASSES and lo <= u[1] and u[2] <= hi]
 
-        def finish(c):
+        def project(j):
+            c = chunks[j][0]
             b, g = divmod(c, PASSES)
-            if g < PASSES - 1:
+            for u in units_of(j):
+                lo, hi = u[1], u[2]
+                if g == 0:
+                    k_accs[u] = psum_k.tile([P, hi - lo], F32, name="k_acc")
+                nc.tensor.matmul_mx(
+                    out=k_accs[u][:],
+                    lhsT=w_codes[:, KW, g, :].bitcast(FP8X4),
+                    lhsT_scale=w_scales[:, KW, g, :],
+                    rhs=x_codes[c][:, lo:hi].bitcast(FP8X4),
+                    rhs_scale=x_scales[c][:, lo:hi],
+                    start=(g == 0),
+                    stop=(g == PASSES - 1),
+                )
+                if g < PASSES - 1:
+                    continue
+                q_acc = psum_q.tile([P, (hi - lo) // P, D], F32, name="q_acc")
+                for s in range((hi - lo) // P):
+                    pixels = slice(lo + s * P, lo + (s + 1) * P)
+                    for h in range(PASSES):
+                        nc.tensor.matmul_mx(
+                            out=q_acc[:, s, :],
+                            lhsT=x_codes[b * PASSES + h][:, pixels].bitcast(FP8X4),
+                            lhsT_scale=x_scales[b * PASSES + h][:, pixels],
+                            rhs=w_codes[:, QW, h, :].bitcast(FP8X4),
+                            rhs_scale=w_scales[:, QW, h, :],
+                            start=(h == 0),
+                            stop=(h == PASSES - 1),
+                        )
+                q_accs[u] = q_acc
+
+        def finish(j):
+            if chunks[j][0] % PASSES < PASSES - 1:
                 return
-            k_out = per_image.tile([P, N], F32, name="k_out")
-            nc.vector.scalar_tensor_tensor(
-                out=k_out[:], in0=k_accs[b][:], scalar=k_bias, in1=gated[:, b, :], op0=ADD, op1=ADD
-            )
-            nc.sync.dma_start(out=out_1[b], in_=k_out[:])
-            q_out = per_image.tile([P, N_TILES, D], F32, name="q_out")
-            nc.vector.tensor_tensor(
-                out=q_out[:],
-                in0=q_accs[b][:],
-                in1=q_bias.unsqueeze(1).to_broadcast([P, N_TILES, D]),
-                op=ADD,
-            )
-            nc.sync.dma_start(out=out_0[b].rearrange("(s p) d -> p s d", p=P), in_=q_out[:])
+            for u in units_of(j):
+                b, lo, hi = u
+                k_out = per_unit.tile([P, hi - lo], F32, name="k_out")
+                nc.vector.scalar_tensor_tensor(
+                    out=k_out[:], in0=k_accs[u][:], scalar=k_bias, in1=gated[:, b, lo:hi], op0=ADD, op1=ADD
+                )
+                nc.sync.dma_start(out=out_1[b][:, lo:hi], in_=k_out[:])
+                q_out = per_unit.tile([P, (hi - lo) // P, D], F32, name="q_out")
+                nc.vector.tensor_tensor(
+                    out=q_out[:],
+                    in0=q_accs[u][:],
+                    in1=q_bias.unsqueeze(1).to_broadcast([P, (hi - lo) // P, D]),
+                    op=ADD,
+                )
+                nc.sync.dma_start(out=out_0[b][lo:hi].rearrange("(s p) d -> p s d", p=P), in_=q_out[:])
 
         regroup(0)
         gate = keep.tile([P, B, HH, WW], F32)
@@ -193,12 +212,12 @@ def tile_self_attn_pa_kernel(tc, x, q_w, q_b, k_w, k_b, a_h, a_w, out_0, out_1):
             out=gated[:], in0=first_channels[:], in1=gate[:].rearrange("p b i j -> p b (i j)"), op=MULT
         )
 
-        for c in range(2, STEPS + 3):
-            if c < STEPS:
-                regroup(c)
-            if c - 1 < STEPS:
-                quantise(c - 1)
-            if c - 2 < STEPS:
-                project(c - 2)
-            if c - 3 >= 0:
-                finish(c - 3)
+        for j in range(2, len(chunks) + 3):
+            if j < len(chunks):
+                regroup(j)
+            if j - 1 < len(chunks):
+                quantise(j - 1)
+            if j - 2 < len(chunks):
+                project(j - 2)
+            if j - 3 >= 0:
+                finish(j - 3)

@@ -22,9 +22,9 @@ N_TILES = N // P
 HALVES = 2
 RUN = 4
 QW, KW = 0, 1
-VECTOR_PIXELS = 128
+VECTOR_PIXELS = 104
 CUTS = {STEPS - 1: (0, N // 2, N)}
-VECTOR_SHARE = {STEPS - 1: 64, STEPS: 64}
+VECTOR_SHARE = {STEPS - 1: 56, STEPS: 48}
 
 FLOPS = 2 * 2 * B * N * D * C
 

@@ -194,26 +194,28 @@ def tile_self_attn_pa_kernel(tc, x, q_w, q_b, k_w, k_b, a_h, a_w, out_0, out_1):
         w_grouped_words = w_grouped[:].bitcast(F32).rearrange(
             "p (w g d u) -> p w g d u", w=2, g=PASSES, u=HALVES
         )
-        for rows, place, copy in ((q_w_rows, QW, nc.scalar.copy), (k_w_rows, KW, nc.scalar.copy)):
-            words = rows[:].bitcast(F32).rearrange("d (g p u) -> d g u p", g=PASSES, u=HALVES)
-            w_t = psum_w.tile([P, PASSES, HALVES, D], F32, name="w_t")
-            for g in range(PASSES):
-                for u in range(HALVES):
-                    nc.tensor.transpose(w_t[:, g, u, :], words[:, g, u, :], identity[:])
-            copy(out=w_grouped_words[:, place], in_=w_t[:].rearrange("p g u d -> p g d u"))
-        nc.vector.quantize_mx(
-            out=w_codes[:].rearrange("p w g d -> p (w g d)").bitcast(FP8X4),
-            scales=w_scales[:].rearrange("p w g d -> p (w g d)"),
-            in_=w_grouped[:],
-        )
-
+        with tc.manual_schedule(engines={mybir.EngineType.Activation}):
+            for rows, place in ((q_w_rows, QW), (k_w_rows, KW)):
+                words = rows[:].bitcast(F32).rearrange("d (g p u) -> d g u p", g=PASSES, u=HALVES)
+                w_t = psum_w.tile([P, PASSES, HALVES, D], F32, name="w_t")
+                for g in range(PASSES):
+                    for u in range(HALVES):
+                        nc.tensor.transpose(w_t[:, g, u, :], words[:, g, u, :], identity[:])
+                nc.scalar.copy(out=w_grouped_words[:, place], in_=w_t[:].rearrange("p g u d -> p g d u"))
+            regroup(2)
         gated = keep.tile([P, B, N], F32)
-        nc.vector.tensor_tensor(
-            out=gated[:], in0=first_channels[:], in1=gate[:].rearrange("p b i j -> p b (i j)"), op=MULT
-        )
+        with tc.manual_schedule(engines={mybir.EngineType.DVE}):
+            nc.vector.quantize_mx(
+                out=w_codes[:].rearrange("p w g d -> p (w g d)").bitcast(FP8X4),
+                scales=w_scales[:].rearrange("p w g d -> p (w g d)"),
+                in_=w_grouped[:],
+            )
+            nc.vector.tensor_tensor(
+                out=gated[:], in0=first_channels[:], in1=gate[:].rearrange("p b i j -> p b (i j)"), op=MULT
+            )
 
         for j in range(2, len(chunks) + 3):
-            if j < len(chunks):
+            if 2 < j < len(chunks):
                 regroup(j)
             if j - 1 < len(chunks):
                 quantise(j - 1)

@@ -26,6 +26,8 @@ VECTOR_PIXELS = 104
 CUTS = {STEPS - 1: (0, N // 2, N)}
 VECTOR_SHARE = {STEPS - 1: 56, STEPS: 48}
 
+LOAD_CUTS = {0: (0, N // 2, N)}
+
 FLOPS = 2 * 2 * B * N * D * C
 
 
@@ -45,8 +47,10 @@ def tile_self_attn_pa_kernel(tc, x, q_w, q_b, k_w, k_b, a_h, a_w, out_0, out_1):
         def load_pass():
             b, g = divmod(len(raws), PASSES)
             raw = per_step.tile([P, PACK, N], BF16, name="raw")
-            channels = x[b, g * K_PASS : (g + 1) * K_PASS]
-            nc.sync.dma_start(out=raw[:], in_=channels.rearrange("(p t) h w -> p t (h w)", t=PACK))
+            channels = x[b, g * K_PASS : (g + 1) * K_PASS].rearrange("(p t) h w -> p t (h w)", t=PACK)
+            cuts = LOAD_CUTS.get(len(raws), (0, N))
+            for lo, hi in zip(cuts[:-1], cuts[1:]):
+                nc.sync.dma_start(out=raw[:, :, lo:hi], in_=channels[:, :, lo:hi])
             raws.append(raw)
 
         load_pass()
@@ -107,7 +111,10 @@ def tile_self_attn_pa_kernel(tc, x, q_w, q_b, k_w, k_b, a_h, a_w, out_0, out_1):
         def regroup(j):
             c, lo, hi = chunks[j]
             cut = lo + VECTOR_SHARE.get(j, VECTOR_PIXELS)
-            for copy, pixels in ((nc.vector.tensor_copy, slice(lo, cut)), (nc.scalar.copy, slice(cut, hi))):
+            shares = [(nc.vector.tensor_copy, slice(lo, cut))]
+            marks = [cut] + [m for m in LOAD_CUTS.get(c, ()) if cut < m < hi] + [hi]
+            shares.extend((nc.scalar.copy, slice(a, z)) for a, z in zip(marks[:-1], marks[1:]))
+            for copy, pixels in shares:
                 if pixels.start == pixels.stop:
                     continue
                 copy(

from contextlib import ExitStack

import concourse.mybir as mybir
from concourse.masks import make_identity

F32 = mybir.dt.float32
BF16 = mybir.dt.bfloat16
U32 = mybir.dt.uint32
U8 = mybir.dt.uint8
FP8X4 = mybir.dt.float8_e4m3fn_x4
ADD = mybir.AluOpType.add
MULT = mybir.AluOpType.mult

P = 128
PACK = 4
K_PASS = P * PACK
B, C, D, HH, WW = 4, 1024, 128, 16, 32
N = HH * WW
PASSES = C // K_PASS
STEPS = B * PASSES
N_TILES = N // P
HALVES = 2
RUN = 4
QW, KW = 0, 1
VECTOR_PIXELS = 104
CUTS = {STEPS - 1: (0, N // 2, N)}
VECTOR_SHARE = {STEPS - 1: 56, STEPS: 48}

LOAD_CUTS = {0: (0, N // 2, N)}

FLOPS = 2 * 2 * B * N * D * C


def tile_self_attn_pa_kernel(tc, x, q_w, q_b, k_w, k_b, a_h, a_w, out_0, out_1):
    nc = tc.nc
    with ExitStack() as ctx:
        keep = ctx.enter_context(tc.tile_pool(name="keep", bufs=1))
        per_step = ctx.enter_context(tc.tile_pool(name="per_step", bufs=STEPS))
        per_unit = ctx.enter_context(tc.tile_pool(name="per_unit", bufs=B + 1))
        psum_w = ctx.enter_context(tc.psum_pool(name="psum_w", bufs=2))
        psum_b = ctx.enter_context(tc.psum_pool(name="psum_b", bufs=1))
        psum_q = ctx.enter_context(tc.psum_pool(name="psum_q", bufs=2))
        psum_k = ctx.enter_context(tc.psum_pool(name="psum_k", bufs=3))

        raws = []

        def load_pass():
            b, g = divmod(len(raws), PASSES)
            raw = per_step.tile([P, PACK, N], BF16, name="raw")
            channels = x[b, g * K_PASS : (g + 1) * K_PASS].rearrange("(p t) h w -> p t (h w)", t=PACK)
            cuts = LOAD_CUTS.get(len(raws), (0, N))
            for lo, hi in zip(cuts[:-1], cuts[1:]):
                nc.sync.dma_start(out=raw[:, :, lo:hi], in_=channels[:, :, lo:hi])
            raws.append(raw)

        load_pass()
        gate_h = keep.tile([P, B, HH], BF16)
        nc.sync.dma_start(out=gate_h[:], in_=a_h.rearrange("b d i -> d b i"))
        gate_w = keep.tile([P, B, WW], BF16)
        nc.sync.dma_start(out=gate_w[:], in_=a_w.rearrange("b d j -> d b j"))
        bias_rows = keep.tile([P, 2, D], BF16)
        nc.gpsimd.memset(bias_rows[:], 0.0)
        nc.sync.dma_start(out=bias_rows[0:1, QW, :], in_=q_b.rearrange("(o d) -> o d", o=1))
        nc.sync.dma_start(out=bias_rows[0:1, KW, :], in_=k_b.rearrange("(o d) -> o d", o=1))
        load_pass()
        q_w_rows = keep.tile([P, C], BF16)
        nc.sync.dma_start(out=q_w_rows[:], in_=q_w)
        k_w_rows = keep.tile([P, C], BF16)
        nc.sync.dma_start(out=k_w_rows[:], in_=k_w)
        load_pass()
        first_channels = keep.tile([P, B, N], BF16)
        nc.sync.dma_start(out=first_channels[:], in_=x[:, 0:D].rearrange("b d h w -> d b (h w)"))
        load_pass()
        for c in range(len(raws), STEPS):
            load_pass()

        identity = keep.tile([P, P], F32)
        make_identity(nc, identity[:])

        ones = keep.tile([P, P], BF16)
        nc.gpsimd.memset(ones[:], 1.0)
        bias_acc = psum_b.tile([P, 2, D], F32)
        nc.tensor.matmul(out=bias_acc[:, QW, :], lhsT=ones[:], rhs=bias_rows[:, QW, :], start=True, stop=True)
        nc.tensor.matmul(out=bias_acc[:, KW, :], lhsT=bias_rows[:, KW, :], rhs=ones[:], start=True, stop=True)
        biases = keep.tile([P, 2, D], F32)
        nc.scalar.copy(out=biases[:], in_=bias_acc[:])
        q_bias = biases[:, QW, :]
        k_bias = biases[:, KW, 0:1]

        chunks = []
        for c in range(STEPS):
            cuts = CUTS.get(c, (0, N))
            chunks.extend((c, lo, hi) for lo, hi in zip(cuts[:-1], cuts[1:]))
        units = []
        for b in range(B):
            cuts = CUTS.get(b * PASSES + PASSES - 1, (0, N))
            units.extend((b, lo, hi) for lo, hi in zip(cuts[:-1], cuts[1:]))

        groupeds = []
        x_codes = []
        x_scales = []
        for c in range(STEPS):
            groupeds.append(per_step.tile([P, N, PACK], BF16, align_bytes=64, name="grouped"))
            x_codes.append(per_step.tile([P, N], U32, align_bytes=64, name="codes"))
            x_scales.append(per_step.tile([P, N], U8, align_bytes=64, name="scales"))
        k_accs = {}
        q_accs = {}
        w_codes = keep.tile([P, 2, PASSES, D], U32, align_bytes=64)
        w_scales = keep.tile([P, 2, PASSES, D], U8, align_bytes=64)

        def regroup(j):
            c, lo, hi = chunks[j]
            cut = lo + VECTOR_SHARE.get(j, VECTOR_PIXELS)
            shares = [(nc.vector.tensor_copy, slice(lo, cut))]
            marks = [cut] + [m for m in LOAD_CUTS.get(c, ()) if cut < m < hi] + [hi]
            shares.extend((nc.scalar.copy, slice(a, z)) for a, z in zip(marks[:-1], marks[1:]))
            for copy, pixels in shares:
                if pixels.start == pixels.stop:
                    continue
                copy(
                    out=groupeds[c][:, pixels, :].rearrange("p (c i) t -> p c t i", i=RUN),
                    in_=raws[c][:, :, pixels].rearrange("p t (c i) -> p c t i", i=RUN),
                )

        def quantise(j):
            c, lo, hi = chunks[j]
            nc.vector.quantize_mx(
                out=x_codes[c][:, lo:hi].bitcast(FP8X4),
                scales=x_scales[c][:, lo:hi],
                in_=groupeds[c][:, lo:hi, :].rearrange("p n t -> p (n t)"),
            )

        def units_of(j):
            c, lo, hi = chunks[j]
            return [u for u in units if u[0] == c // PASSES and lo <= u[1] and u[2] <= hi]

        def project(j):
            c = chunks[j][0]
            b, g = divmod(c, PASSES)
            for u in units_of(j):
                lo, hi = u[1], u[2]
                if g == 0:
                    k_accs[u] = psum_k.tile([P, hi - lo], F32, name="k_acc")
                nc.tensor.matmul_mx(
                    out=k_accs[u][:],
                    lhsT=w_codes[:, KW, g, :].bitcast(FP8X4),
                    lhsT_scale=w_scales[:, KW, g, :],
                    rhs=x_codes[c][:, lo:hi].bitcast(FP8X4),
                    rhs_scale=x_scales[c][:, lo:hi],
                    start=(g == 0),
                    stop=(g == PASSES - 1),
                )
                if g < PASSES - 1:
                    continue
                q_acc = psum_q.tile([P, (hi - lo) // P, D], F32, name="q_acc")
                for s in range((hi - lo) // P):
                    pixels = slice(lo + s * P, lo + (s + 1) * P)
                    for h in range(PASSES):
                        nc.tensor.matmul_mx(
                            out=q_acc[:, s, :],
                            lhsT=x_codes[b * PASSES + h][:, pixels].bitcast(FP8X4),
                            lhsT_scale=x_scales[b * PASSES + h][:, pixels],
                            rhs=w_codes[:, QW, h, :].bitcast(FP8X4),
                            rhs_scale=w_scales[:, QW, h, :],
                            start=(h == 0),
                            stop=(h == PASSES - 1),
                        )
                q_accs[u] = q_acc

        def finish(j):
            if chunks[j][0] % PASSES < PASSES - 1:
                return
            for u in units_of(j):
                b, lo, hi = u
                k_out = per_unit.tile([P, hi - lo], F32, name="k_out")
                nc.vector.scalar_tensor_tensor(
                    out=k_out[:], in0=k_accs[u][:], scalar=k_bias, in1=gated[:, b, lo:hi], op0=ADD, op1=ADD
                )
                nc.sync.dma_start(out=out_1[b][:, lo:hi], in_=k_out[:])
                q_out = per_unit.tile([P, (hi - lo) // P, D], F32, name="q_out")
                nc.vector.tensor_tensor(
                    out=q_out[:],
                    in0=q_accs[u][:],
                    in1=q_bias.unsqueeze(1).to_broadcast([P, (hi - lo) // P, D]),
                    op=ADD,
                )
                nc.sync.dma_start(out=out_0[b][lo:hi].rearrange("(s p) d -> p s d", p=P), in_=q_out[:])

        regroup(0)
        gate = keep.tile([P, B, HH, WW], F32)
        nc.vector.tensor_tensor(
            out=gate[:],
            in0=gate_h[:].unsqueeze(3).to_broadcast([P, B, HH, WW]),
            in1=gate_w[:].unsqueeze(2).to_broadcast([P, B, HH, WW]),
            op=MULT,
        )
        regroup(1)
        quantise(0)

        w_grouped = keep.tile([P, 2 * PASSES * D * PACK], BF16, align_bytes=64)
        w_grouped_words = w_grouped[:].bitcast(F32).rearrange(
            "p (w g d u) -> p w g d u", w=2, g=PASSES, u=HALVES
        )
        with tc.manual_schedule(engines={mybir.EngineType.Activation}):
            for rows, place in ((q_w_rows, QW), (k_w_rows, KW)):
                words = rows[:].bitcast(F32).rearrange("d (g p u) -> d g u p", g=PASSES, u=HALVES)
                w_t = psum_w.tile([P, PASSES, HALVES, D], F32, name="w_t")
                for g in range(PASSES):
                    for u in range(HALVES):
                        nc.tensor.transpose(w_t[:, g, u, :], words[:, g, u, :], identity[:])
                nc.scalar.copy(out=w_grouped_words[:, place], in_=w_t[:].rearrange("p g u d -> p g d u"))
            regroup(2)
        gated = keep.tile([P, B, N], F32)
        with tc.manual_schedule(engines={mybir.EngineType.DVE}):
            nc.vector.quantize_mx(
                out=w_codes[:].rearrange("p w g d -> p (w g d)").bitcast(FP8X4),
                scales=w_scales[:].rearrange("p w g d -> p (w g d)"),
                in_=w_grouped[:],
            )
            nc.vector.tensor_tensor(
                out=gated[:], in0=first_channels[:], in1=gate[:].rearrange("p b i j -> p b (i j)"), op=MULT
            )

        for j in range(2, len(chunks) + 3):
            if 2 < j < len(chunks):
                regroup(j)
            if j - 1 < len(chunks):
                quantise(j - 1)
            if j - 2 < len(chunks):
                project(j - 2)
            if j - 3 >= 0:
                finish(j - 3)
